import numpy as np
import ml_dtypes


def mxq(x, axis, fmt="e4m3"):
    dtype, down = {"e4m3": (ml_dtypes.float8_e4m3fn, 7), "e5m2": (ml_dtypes.float8_e5m2, 14)}[fmt]
    v = np.moveaxis(np.asarray(x, np.float32).astype(ml_dtypes.bfloat16).astype(np.float64), axis, -1)
    blocks = v.reshape(v.shape[:-1] + (-1, 32))
    amax = np.abs(blocks).max(-1, keepdims=True)
    byte = np.maximum(np.where(amax > 0, np.frexp(amax)[1] - 1 + 127, 0) - down, 1)
    scale = np.exp2(byte - 127.0)
    codes = (blocks / scale).astype(np.float32).astype(dtype).astype(np.float64)
    return np.moveaxis((codes * scale).reshape(v.shape), -1, axis)


WIDE = False


def mx_kscale(k):
    if not WIDE:
        return np.ones(k)
    levels = np.array([10, -10, 5, -5, 0])
    a = np.random.permutation(np.resize(levels, k // 512 * 4)).reshape(k // 512, 4)
    idx = np.arange(k)
    return np.exp2(a[idx // 512, idx % 128 // 32])


BF16 = ml_dtypes.bfloat16


def bf(x):
    return np.asarray(x, np.float32).astype(BF16)


def f64(x):
    return np.asarray(x).astype(np.float64)


N, G, F, K, E = 512, 4096, 128, 4, 1


def setup_inputs():
    s = mx_kscale(N)
    return {"x": bf(np.random.standard_normal((N, G)) * s[:, None]),
            "S": bf(np.random.standard_normal((E, N, N)) / np.sqrt(N) / s[:, None] * s[None, :])}


def reference(x, S):
    Sq = mxq(f64(S), 1, "e4m3")
    z0 = np.broadcast_to(f64(x).T[None], (E, G, N))
    z1 = mxq(z0, 2, "e4m3") @ Sq
    z2 = mxq(z1, 2, "e4m3") @ Sq
    return z1, z2

@@ -1,0 +1,183 @@
+from contextlib import ExitStack
+
+import concourse.mybir as mybir
+
+F32 = mybir.dt.float32
+BF16 = mybir.dt.bfloat16
+U32 = mybir.dt.uint32
+U8 = mybir.dt.uint8
+FP8X4 = mybir.dt.float8_e4m3fn_x4
+
+P = 128
+PACK = 4
+NODES = 512
+FEATS = 4096
+CHUNK = 512
+ROWS = 4
+NCHUNK = FEATS // CHUNK
+LOAD_WIDTHS = (512, 512, 1024, 2048)
+FLOPS = 2 * 2 * FEATS * NODES * NODES
+
+
+def tile_graphfilter_pa_t_kernel(tc, x, S, out_0, out_1):
+    nc = tc.nc
+    x_view = x.rearrange("(t p) g -> p t g", p=P)
+    s_view = S[0, :, :].rearrange("(t p) n -> p t n", p=P)
+    z1_view = out_0[0, :, :].rearrange("(c m r) j -> c m r j", m=P, r=ROWS)
+    z2_view = out_1[0, :, :].rearrange("(c m r) j -> c m r j", m=P, r=ROWS)
+
+    with ExitStack() as ctx:
+        keep = ctx.enter_context(tc.tile_pool(name="keep", bufs=1))
+        grp = ctx.enter_context(tc.tile_pool(name="grp", bufs=3))
+        stage = ctx.enter_context(tc.tile_pool(name="stage", bufs=8))
+        psum_t = ctx.enter_context(tc.psum_pool(name="psum_t", bufs=4))
+        psum_o = ctx.enter_context(tc.psum_pool(name="psum_o", bufs=4))
+        ctx.enter_context(tc.manual_schedule())
+
+        s_raw = keep.tile([P, PACK, NODES], BF16, name="s_raw")
+        nc.sync.dma_start(out=s_raw[:], in_=s_view)
+        x_raw = []
+        start = 0
+        for i, width in enumerate(LOAD_WIDTHS):
+            raw = keep.tile([P, PACK, width], BF16, name="x_raw%d" % i)
+            nc.sync.dma_start(out=raw[:], in_=x_view[:, :, start : start + width])
+            for k in range(width // CHUNK):
+                x_raw.append(raw[:, :, k * CHUNK : (k + 1) * CHUNK])
+            start += width
+
+        s_grp = keep.tile([P, NODES, PACK], BF16, name="s_grp", align_bytes=64)
+        s_codes = keep.tile([P, NODES], U32, name="s_codes", align_bytes=64)
+        s_scales = keep.tile([P, NODES], U8, name="s_scales", align_bytes=64)
+
+        x_grp = {}
+        x_codes = {}
+        x_scales = {}
+        z_grp = {}
+        z_codes = {}
+        z_scales = {}
+        zt_bank = {}
+        out_bank = {}
+        out_stage = {}
+
+        def regroup_x(c):
+            x_grp[c] = grp.tile([P, ROWS, P, PACK], BF16, name="x_grp%d" % c, tag="x_grp", align_bytes=64)
+            nc.vector.tensor_copy(
+                out=x_grp[c][:],
+                in_=x_raw[c].rearrange("p t (m r) -> p r m t", r=ROWS),
+            )
+
+        def quantise_x(c):
+            x_codes[c] = keep.tile([P, CHUNK], U32, name="x_codes%d" % c, align_bytes=64)
+            x_scales[c] = keep.tile([P, CHUNK], U8, name="x_scales%d" % c, align_bytes=64)
+            nc.vector.quantize_mx(
+                out=x_codes[c][:].bitcast(FP8X4),
+                scales=x_scales[c][:],
+                in_=x_grp[c][:].rearrange("p r m t -> p (r m t)"),
+            )
+
+        def shift_transposed(c, r):
+            cols = slice(r * P, (r + 1) * P)
+            bank = psum_t.tile([P, PACK, P], F32, name="zt%d_%d" % (c, r), tag="zt")
+            zt_bank[(c, r)] = bank
+            for t in range(PACK):
+                nodes = slice(t * P, (t + 1) * P)
+                nc.tensor.matmul_mx(
+                    out=bank[:, t, :],
+                    lhsT=s_codes[:, nodes].bitcast(FP8X4),
+                    lhsT_scale=s_scales[:, nodes],
+                    rhs=x_codes[c][:, cols].bitcast(FP8X4),
+                    rhs_scale=x_scales[c][:, cols],
+                    start=True,
+                    stop=True,
+                )
+
+        def shift(which, codes, scales, c, r):
+            cols = slice(r * P, (r + 1) * P)
+            bank = psum_o.tile([P, NODES], F32, name="zo%d_%d_%d" % (which, c, r), tag="zo")
+            out_bank[(which, c, r)] = bank
+            nc.tensor.matmul_mx(
+                out=bank[:],
+                lhsT=codes[c][:, cols].bitcast(FP8X4),
+                lhsT_scale=scales[c][:, cols],
+                rhs=s_codes[:].bitcast(FP8X4),
+                rhs_scale=s_scales[:],
+                start=True,
+                stop=True,
+            )
+
+        def regroup_z(c, r):
+            if r == 0:
+                z_grp[c] = grp.tile([P, ROWS, P, PACK], BF16, name="z_grp%d" % c, tag="z_grp", align_bytes=64)
+            nc.vector.tensor_copy(
+                out=z_grp[c][:, r, :, :],
+                in_=zt_bank[(c, r)][:].rearrange("p t g -> p g t"),
+            )
+
+        def quantise_z(c):
+            z_codes[c] = keep.tile([P, CHUNK], U32, name="z_codes%d" % c, align_bytes=64)
+            z_scales[c] = keep.tile([P, CHUNK], U8, name="z_scales%d" % c, align_bytes=64)
+            nc.vector.quantize_mx(
+                out=z_codes[c][:].bitcast(FP8X4),
+                scales=z_scales[c][:],
+                in_=z_grp[c][:].rearrange("p r m t -> p (r m t)"),
+            )
+
+        def empty(which, c, r, engine):
+            if r == 0:
+                out_stage[(which, c)] = stage.tile([P, ROWS, NODES], F32, name="st%d_%d" % (which, c), tag="st")
+            dst = out_stage[(which, c)][:, r, :]
+            src = out_bank[(which, c, r)][:]
+            if engine == "scalar":
+                nc.scalar.copy(out=dst, in_=src)
+            else:
+                nc.vector.tensor_copy(out=dst, in_=src)
+
+        def store(which, c, lo, hi):
+            view = z1_view if which == 1 else z2_view
+            nc.sync.dma_start(out=view[c][:, lo:hi, :], in_=out_stage[(which, c)][:, lo:hi, :])
+
+        nc.vector.tensor_copy(out=s_grp[:], in_=s_raw[:].rearrange("p t n -> p n t"))
+        regroup_x(0)
+        nc.vector.quantize_mx(
+            out=s_codes[:].bitcast(FP8X4),
+            scales=s_scales[:],
+            in_=s_grp[:].rearrange("p n t -> p (n t)"),
+        )
+        quantise_x(0)
+
+        for c in range(NCHUNK):
+            shift_transposed(c, 0)
+            shift_transposed(c, 1)
+            shift(1, x_codes, x_scales, c, 0)
+            shift(1, x_codes, x_scales, c, 1)
+            shift_transposed(c, 2)
+            shift_transposed(c, 3)
+            shift(1, x_codes, x_scales, c, 2)
+            shift(1, x_codes, x_scales, c, 3)
+
+            if c + 1 < NCHUNK:
+                regroup_x(c + 1)
+            for r in range(ROWS):
+                regroup_z(c, r)
+            if c + 1 < NCHUNK:
+                quantise_x(c + 1)
+            quantise_z(c)
+
+            for r in range(ROWS):
+                empty(1, c, r, "scalar")
+            store(1, c, 0, ROWS)
+            if c > 0:
+                for r in range(ROWS):
+                    shift(2, z_codes, z_scales, c - 1, r)
+                    empty(2, c - 1, r, "scalar")
+                store(2, c - 1, 0, ROWS)
+
+        last = NCHUNK - 1
+        for r in range(ROWS):
+            shift(2, z_codes, z_scales, last, r)
+        empty(2, last, 0, "scalar")
+        empty(2, last, 1, "vector")
+        store(2, last, 0, 2)
+        empty(2, last, 2, "scalar")
+        empty(2, last, 3, "vector")
+        store(2, last, 2, 4)

@@ -62,8 +62,8 @@ def tile_graphfilter_pa_t_kernel(tc, x, S, out_0, out_1):
         def regroup_x(c):
             x_grp[c] = grp.tile([P, ROWS, P, PACK], BF16, name="x_grp%d" % c, tag="x_grp", align_bytes=64)
             nc.vector.tensor_copy(
-                out=x_grp[c][:],
-                in_=x_raw[c].rearrange("p t (m r) -> p r m t", r=ROWS),
+                out=x_grp[c][:].rearrange("p r m t -> p m t r"),
+                in_=x_raw[c].rearrange("p t (m r) -> p m t r", r=ROWS),
             )
 
         def quantise_x(c):

@@ -59,12 +59,20 @@ def tile_graphfilter_pa_t_kernel(tc, x, S, out_0, out_1):
         out_bank = {}
         out_stage = {}
 
-        def regroup_x(c):
-            x_grp[c] = grp.tile([P, ROWS, P, PACK], BF16, name="x_grp%d" % c, tag="x_grp", align_bytes=64)
-            nc.vector.tensor_copy(
-                out=x_grp[c][:].rearrange("p r m t -> p m t r"),
-                in_=x_raw[c].rearrange("p t (m r) -> p m t r", r=ROWS),
-            )
+        def regroup_x(c, engine):
+            tag = "x_grp" if c >= 2 else "x_grp%d" % c
+            x_grp[c] = keep.tile([P, ROWS, P, PACK], BF16, name="x_grp_%d" % c, tag=tag, align_bytes=64)
+            dst = x_grp[c][:].rearrange("p r m t -> p m t r")
+            src = x_raw[c].rearrange("p t (m r) -> p m t r", r=ROWS)
+            if engine == "vector":
+                nc.vector.tensor_copy(out=dst, in_=src)
+            elif engine == "scalar":
+                nc.scalar.copy(out=dst, in_=src)
+            else:
+                nc.gpsimd.tensor_scalar(
+                    out=dst, in0=src, scalar1=1.0, scalar2=0.0,
+                    op0=mybir.AluOpType.mult, op1=mybir.AluOpType.add,
+                )
 
         def quantise_x(c):
             x_codes[c] = keep.tile([P, CHUNK], U32, name="x_codes%d" % c, align_bytes=64)
@@ -137,40 +145,61 @@ def tile_graphfilter_pa_t_kernel(tc, x, S, out_0, out_1):
             nc.sync.dma_start(out=view[c][:, lo:hi, :], in_=out_stage[(which, c)][:, lo:hi, :])
 
         nc.vector.tensor_copy(out=s_grp[:], in_=s_raw[:].rearrange("p t n -> p n t"))
-        regroup_x(0)
+        regroup_x(0, "vector")
+        regroup_x(1, "scalar")
         nc.vector.quantize_mx(
             out=s_codes[:].bitcast(FP8X4),
             scales=s_scales[:],
             in_=s_grp[:].rearrange("p n t -> p (n t)"),
         )
         quantise_x(0)
+        regroup_x(2, "gpsimd")
+        for r in range(ROWS):
+            shift_transposed(0, r)
+        for r in range(ROWS):
+            shift(1, x_codes, x_scales, 0, r)
 
-        for c in range(NCHUNK):
-            shift_transposed(c, 0)
-            shift_transposed(c, 1)
-            shift(1, x_codes, x_scales, c, 0)
-            shift(1, x_codes, x_scales, c, 1)
-            shift_transposed(c, 2)
-            shift_transposed(c, 3)
-            shift(1, x_codes, x_scales, c, 2)
-            shift(1, x_codes, x_scales, c, 3)
+        for r in range(ROWS):
+            regroup_z(0, r)
+        empty(1, 0, 0, "scalar")
+        empty(1, 0, 1, "scalar")
+        empty(1, 0, 2, "vector")
+        empty(1, 0, 3, "vector")
+        store(1, 0, 0, ROWS)
+        quantise_x(1)
+        quantise_z(0)
+        quantise_x(2)
+        regroup_x(3, "gpsimd")
+        for r in range(ROWS):
+            shift_transposed(1, r)
+        shift(1, x_codes, x_scales, 1, 0)
 
-            if c + 1 < NCHUNK:
-                regroup_x(c + 1)
+        for c in range(1, NCHUNK):
+            for r in range(3):
+                shift(2, z_codes, z_scales, c - 1, r)
+            empty(1, c, 0, "scalar")
+            for r in range(3):
+                empty(2, c - 1, r, "scalar")
             for r in range(ROWS):
                 regroup_z(c, r)
-            if c + 1 < NCHUNK:
-                quantise_x(c + 1)
-            quantise_z(c)
-
-            for r in range(ROWS):
+                if c + 1 < NCHUNK:
+                    shift_transposed(c + 1, r)
+                if r == 0:
+                    shift(2, z_codes, z_scales, c - 1, 3)
+                else:
+                    shift(1, x_codes, x_scales, c, r)
+            empty(2, c - 1, 3, "vector")
+            store(2, c - 1, 0, ROWS)
+            for r in range(1, ROWS):
                 empty(1, c, r, "scalar")
             store(1, c, 0, ROWS)
-            if c > 0:
-                for r in range(ROWS):
-                    shift(2, z_codes, z_scales, c - 1, r)
-                    empty(2, c - 1, r, "scalar")
-                store(2, c - 1, 0, ROWS)
+            quantise_z(c)
+            if c + 2 < NCHUNK:
+                quantise_x(c + 2)
+            if c + 3 < NCHUNK:
+                regroup_x(c + 3, "gpsimd")
+            if c + 1 < NCHUNK:
+                shift(1, x_codes, x_scales, c + 1, 0)
 
         last = NCHUNK - 1
         for r in range(ROWS):

@@ -35,12 +35,13 @@ def tile_graphfilter_pa_t_kernel(tc, x, S, out_0, out_1):
         ctx.enter_context(tc.manual_schedule())
 
         s_raw = keep.tile([P, PACK, NODES], BF16, name="s_raw")
-        nc.sync.dma_start(out=s_raw[:], in_=s_view)
         x_raw = []
         start = 0
         for i, width in enumerate(LOAD_WIDTHS):
             raw = keep.tile([P, PACK, width], BF16, name="x_raw%d" % i)
             nc.sync.dma_start(out=raw[:], in_=x_view[:, :, start : start + width])
+            if i == 0:
+                nc.sync.dma_start(out=s_raw[:], in_=s_view)
             for k in range(width // CHUNK):
                 x_raw.append(raw[:, :, k * CHUNK : (k + 1) * CHUNK])
             start += width
@@ -59,11 +60,12 @@ def tile_graphfilter_pa_t_kernel(tc, x, S, out_0, out_1):
         out_bank = {}
         out_stage = {}
 
-        def regroup_x(c, engine):
-            tag = "x_grp" if c >= 2 else "x_grp%d" % c
-            x_grp[c] = keep.tile([P, ROWS, P, PACK], BF16, name="x_grp_%d" % c, tag=tag, align_bytes=64)
-            dst = x_grp[c][:].rearrange("p r m t -> p m t r")
-            src = x_raw[c].rearrange("p t (m r) -> p m t r", r=ROWS)
+        def regroup_x(c, engine, lo, hi):
+            if c not in x_grp:
+                tag = "x_grp" if c >= 1 else "x_grp0"
+                x_grp[c] = keep.tile([P, ROWS, P, PACK], BF16, name="x_grp_%d" % c, tag=tag, align_bytes=64)
+            dst = x_grp[c][:, :, lo:hi, :].rearrange("p r m t -> p m t r")
+            src = x_raw[c][:, :, ROWS * lo : ROWS * hi].rearrange("p t (m r) -> p m t r", r=ROWS)
             if engine == "vector":
                 nc.vector.tensor_copy(out=dst, in_=src)
             elif engine == "scalar":
@@ -131,7 +133,7 @@ def tile_graphfilter_pa_t_kernel(tc, x, S, out_0, out_1):
             )
 
         def empty(which, c, r, engine):
-            if r == 0:
+            if (which, c) not in out_stage:
                 out_stage[(which, c)] = stage.tile([P, ROWS, NODES], F32, name="st%d_%d" % (which, c), tag="st")
             dst = out_stage[(which, c)][:, r, :]
             src = out_bank[(which, c, r)][:]
@@ -144,62 +146,66 @@ def tile_graphfilter_pa_t_kernel(tc, x, S, out_0, out_1):
             view = z1_view if which == 1 else z2_view
             nc.sync.dma_start(out=view[c][:, lo:hi, :], in_=out_stage[(which, c)][:, lo:hi, :])
 
-        nc.vector.tensor_copy(out=s_grp[:], in_=s_raw[:].rearrange("p t n -> p n t"))
-        regroup_x(0, "vector")
-        regroup_x(1, "scalar")
+        HALF = NODES // 2
+        SPLIT = 80
+        regroup_x(0, "vector", 0, P)
+        nc.vector.tensor_copy(out=s_grp[:, :HALF, :], in_=s_raw[:, :, :HALF].rearrange("p t n -> p n t"))
+        nc.scalar.copy(out=s_grp[:, HALF:, :], in_=s_raw[:, :, HALF:].rearrange("p t n -> p n t"))
+        quantise_x(0)
         nc.vector.quantize_mx(
             out=s_codes[:].bitcast(FP8X4),
             scales=s_scales[:],
             in_=s_grp[:].rearrange("p n t -> p (n t)"),
         )
-        quantise_x(0)
-        regroup_x(2, "gpsimd")
+        regroup_x(1, "scalar", 0, P)
         for r in range(ROWS):
             shift_transposed(0, r)
-        for r in range(ROWS):
             shift(1, x_codes, x_scales, 0, r)
 
-        for r in range(ROWS):
-            regroup_z(0, r)
-        empty(1, 0, 0, "scalar")
-        empty(1, 0, 1, "scalar")
-        empty(1, 0, 2, "vector")
-        empty(1, 0, 3, "vector")
-        store(1, 0, 0, ROWS)
+        regroup_z(0, 0)
         quantise_x(1)
+        regroup_x(2, "gpsimd", 0, SPLIT)
+        for r in range(ROWS):
+            empty(1, 0, r, "scalar")
+        store(1, 0, 0, ROWS)
+        for r in range(ROWS):
+            if r > 0:
+                regroup_z(0, r)
+            shift_transposed(1, r)
+            shift(1, x_codes, x_scales, 1, r)
+        for r in range(ROWS):
+            empty(1, 1, r, "scalar")
+        store(1, 1, 0, ROWS)
+        regroup_x(2, "vector", SPLIT, P)
         quantise_z(0)
         quantise_x(2)
-        regroup_x(3, "gpsimd")
-        for r in range(ROWS):
-            shift_transposed(1, r)
-        shift(1, x_codes, x_scales, 1, 0)
 
         for c in range(1, NCHUNK):
-            for r in range(3):
+            if c + 2 < NCHUNK:
+                regroup_x(c + 2, "gpsimd", 0, SPLIT)
+            for r in range(ROWS):
                 shift(2, z_codes, z_scales, c - 1, r)
-            empty(1, c, 0, "scalar")
-            for r in range(3):
+            for r in range(ROWS):
                 empty(2, c - 1, r, "scalar")
+            store(2, c - 1, 0, ROWS)
             for r in range(ROWS):
                 regroup_z(c, r)
                 if c + 1 < NCHUNK:
                     shift_transposed(c + 1, r)
-                if r == 0:
-                    shift(2, z_codes, z_scales, c - 1, 3)
-                else:
-                    shift(1, x_codes, x_scales, c, r)
-            empty(2, c - 1, 3, "vector")
-            store(2, c - 1, 0, ROWS)
-            for r in range(1, ROWS):
-                empty(1, c, r, "scalar")
-            store(1, c, 0, ROWS)
+                    shift(1, x_codes, x_scales, c + 1, r)
+            if c + 1 < NCHUNK:
+                helped = c % 2 == 0
+                if helped:
+                    empty(1, c + 1, 0, "vector")
+                for r in range(ROWS):
+                    if not (helped and r == 0):
+                        empty(1, c + 1, r, "scalar")
+                store(1, c + 1, 0, ROWS)
+            if c + 2 < NCHUNK:
+                regroup_x(c + 2, "vector", SPLIT, P)
             quantise_z(c)
             if c + 2 < NCHUNK:
                 quantise_x(c + 2)
-            if c + 3 < NCHUNK:
-                regroup_x(c + 3, "gpsimd")
-            if c + 1 < NCHUNK:
-                shift(1, x_codes, x_scales, c + 1, 0)
 
         last = NCHUNK - 1
         for r in range(ROWS):

@@ -157,14 +157,15 @@ def tile_graphfilter_pa_t_kernel(tc, x, S, out_0, out_1):
             scales=s_scales[:],
             in_=s_grp[:].rearrange("p n t -> p (n t)"),
         )
-        regroup_x(1, "scalar", 0, P)
+        regroup_x(1, "scalar", 0, 64)
+        regroup_x(1, "vector", 64, P)
         for r in range(ROWS):
             shift_transposed(0, r)
             shift(1, x_codes, x_scales, 0, r)
 
         regroup_z(0, 0)
         quantise_x(1)
-        regroup_x(2, "gpsimd", 0, SPLIT)
+        regroup_x(2, "gpsimd", 0, 48)
         for r in range(ROWS):
             empty(1, 0, r, "scalar")
         store(1, 0, 0, ROWS)
@@ -176,8 +177,8 @@ def tile_graphfilter_pa_t_kernel(tc, x, S, out_0, out_1):
         for r in range(ROWS):
             empty(1, 1, r, "scalar")
         store(1, 1, 0, ROWS)
-        regroup_x(2, "vector", SPLIT, P)
         quantise_z(0)
+        regroup_x(2, "vector", 48, P)
         quantise_x(2)
 
         for c in range(1, NCHUNK):

@@ -147,7 +147,7 @@ def tile_graphfilter_pa_t_kernel(tc, x, S, out_0, out_1):
             nc.sync.dma_start(out=view[c][:, lo:hi, :], in_=out_stage[(which, c)][:, lo:hi, :])
 
         HALF = NODES // 2
-        SPLIT = 80
+        SPLIT = 96
         regroup_x(0, "vector", 0, P)
         nc.vector.tensor_copy(out=s_grp[:, :HALF, :], in_=s_raw[:, :, :HALF].rearrange("p t n -> p n t"))
         nc.scalar.copy(out=s_grp[:, HALF:, :], in_=s_raw[:, :, HALF:].rearrange("p t n -> p n t"))
@@ -195,7 +195,7 @@ def tile_graphfilter_pa_t_kernel(tc, x, S, out_0, out_1):
                     shift_transposed(c + 1, r)
                     shift(1, x_codes, x_scales, c + 1, r)
             if c + 1 < NCHUNK:
-                helped = c % 2 == 0
+                helped = True
                 if helped:
                     empty(1, c + 1, 0, "vector")
                 for r in range(ROWS):
@@ -213,7 +213,6 @@ def tile_graphfilter_pa_t_kernel(tc, x, S, out_0, out_1):
             shift(2, z_codes, z_scales, last, r)
         empty(2, last, 0, "scalar")
         empty(2, last, 1, "vector")
-        store(2, last, 0, 2)
         empty(2, last, 2, "scalar")
         empty(2, last, 3, "vector")
-        store(2, last, 2, 4)
+        store(2, last, 0, ROWS)

@@ -147,7 +147,7 @@ def tile_graphfilter_pa_t_kernel(tc, x, S, out_0, out_1):
             nc.sync.dma_start(out=view[c][:, lo:hi, :], in_=out_stage[(which, c)][:, lo:hi, :])
 
         HALF = NODES // 2
-        SPLIT = 96
+        SPLIT = 80
         regroup_x(0, "vector", 0, P)
         nc.vector.tensor_copy(out=s_grp[:, :HALF, :], in_=s_raw[:, :, :HALF].rearrange("p t n -> p n t"))
         nc.scalar.copy(out=s_grp[:, HALF:, :], in_=s_raw[:, :, HALF:].rearrange("p t n -> p n t"))
@@ -183,7 +183,7 @@ def tile_graphfilter_pa_t_kernel(tc, x, S, out_0, out_1):
 
         for c in range(1, NCHUNK):
             if c + 2 < NCHUNK:
-                regroup_x(c + 2, "gpsimd", 0, SPLIT)
+                regroup_x(c + 2, "gpsimd", 0, (104 if c % 2 == 0 else SPLIT))
             for r in range(ROWS):
                 shift(2, z_codes, z_scales, c - 1, r)
             for r in range(ROWS):
@@ -195,7 +195,7 @@ def tile_graphfilter_pa_t_kernel(tc, x, S, out_0, out_1):
                     shift_transposed(c + 1, r)
                     shift(1, x_codes, x_scales, c + 1, r)
             if c + 1 < NCHUNK:
-                helped = True
+                helped = c % 2 == 0
                 if helped:
                     empty(1, c + 1, 0, "vector")
                 for r in range(ROWS):
@@ -203,7 +203,7 @@ def tile_graphfilter_pa_t_kernel(tc, x, S, out_0, out_1):
                         empty(1, c + 1, r, "scalar")
                 store(1, c + 1, 0, ROWS)
             if c + 2 < NCHUNK:
-                regroup_x(c + 2, "vector", SPLIT, P)
+                regroup_x(c + 2, "vector", (104 if c % 2 == 0 else SPLIT), P)
             quantise_z(c)
             if c + 2 < NCHUNK:
                 quantise_x(c + 2)
@@ -213,6 +213,7 @@ def tile_graphfilter_pa_t_kernel(tc, x, S, out_0, out_1):
             shift(2, z_codes, z_scales, last, r)
         empty(2, last, 0, "scalar")
         empty(2, last, 1, "vector")
+        store(2, last, 0, 2)
         empty(2, last, 2, "scalar")
         empty(2, last, 3, "vector")
-        store(2, last, 0, ROWS)
+        store(2, last, 2, 4)

from contextlib import ExitStack

import concourse.mybir as mybir

F32 = mybir.dt.float32
BF16 = mybir.dt.bfloat16
U32 = mybir.dt.uint32
U8 = mybir.dt.uint8
FP8X4 = mybir.dt.float8_e4m3fn_x4

P = 128
PACK = 4
NODES = 512
FEATS = 4096
CHUNK = 512
ROWS = 4
NCHUNK = FEATS // CHUNK
LOAD_WIDTHS = (512, 512, 1024, 2048)
FLOPS = 2 * 2 * FEATS * NODES * NODES


def tile_graphfilter_pa_t_kernel(tc, x, S, out_0, out_1):
    nc = tc.nc
    x_view = x.rearrange("(t p) g -> p t g", p=P)
    s_view = S[0, :, :].rearrange("(t p) n -> p t n", p=P)
    z1_view = out_0[0, :, :].rearrange("(c m r) j -> c m r j", m=P, r=ROWS)
    z2_view = out_1[0, :, :].rearrange("(c m r) j -> c m r j", m=P, r=ROWS)

    with ExitStack() as ctx:
        keep = ctx.enter_context(tc.tile_pool(name="keep", bufs=1))
        grp = ctx.enter_context(tc.tile_pool(name="grp", bufs=3))
        stage = ctx.enter_context(tc.tile_pool(name="stage", bufs=8))
        psum_t = ctx.enter_context(tc.psum_pool(name="psum_t", bufs=4))
        psum_o = ctx.enter_context(tc.psum_pool(name="psum_o", bufs=4))
        ctx.enter_context(tc.manual_schedule())

        s_raw = keep.tile([P, PACK, NODES], BF16, name="s_raw")
        x_raw = []
        start = 0
        for i, width in enumerate(LOAD_WIDTHS):
            raw = keep.tile([P, PACK, width], BF16, name="x_raw%d" % i)
            nc.sync.dma_start(out=raw[:], in_=x_view[:, :, start : start + width])
            if i == 0:
                nc.sync.dma_start(out=s_raw[:], in_=s_view)
            for k in range(width // CHUNK):
                x_raw.append(raw[:, :, k * CHUNK : (k + 1) * CHUNK])
            start += width

        s_grp = keep.tile([P, NODES, PACK], BF16, name="s_grp", align_bytes=64)
        s_codes = keep.tile([P, NODES], U32, name="s_codes", align_bytes=64)
        s_scales = keep.tile([P, NODES], U8, name="s_scales", align_bytes=64)

        x_grp = {}
        x_codes = {}
        x_scales = {}
        z_grp = {}
        z_codes = {}
        z_scales = {}
        zt_bank = {}
        out_bank = {}
        out_stage = {}

        def regroup_x(c, engine, lo, hi):
            if c not in x_grp:
                tag = "x_grp" if c >= 1 else "x_grp0"
                x_grp[c] = keep.tile([P, ROWS, P, PACK], BF16, name="x_grp_%d" % c, tag=tag, align_bytes=64)
            dst = x_grp[c][:, :, lo:hi, :].rearrange("p r m t -> p m t r")
            src = x_raw[c][:, :, ROWS * lo : ROWS * hi].rearrange("p t (m r) -> p m t r", r=ROWS)
            if engine == "vector":
                nc.vector.tensor_copy(out=dst, in_=src)
            elif engine == "scalar":
                nc.scalar.copy(out=dst, in_=src)
            else:
                nc.gpsimd.tensor_scalar(
                    out=dst, in0=src, scalar1=1.0, scalar2=0.0,
                    op0=mybir.AluOpType.mult, op1=mybir.AluOpType.add,
                )

        def quantise_x(c):
            x_codes[c] = keep.tile([P, CHUNK], U32, name="x_codes%d" % c, align_bytes=64)
            x_scales[c] = keep.tile([P, CHUNK], U8, name="x_scales%d" % c, align_bytes=64)
            nc.vector.quantize_mx(
                out=x_codes[c][:].bitcast(FP8X4),
                scales=x_scales[c][:],
                in_=x_grp[c][:].rearrange("p r m t -> p (r m t)"),
            )

        def shift_transposed(c, r):
            cols = slice(r * P, (r + 1) * P)
            bank = psum_t.tile([P, PACK, P], F32, name="zt%d_%d" % (c, r), tag="zt")
            zt_bank[(c, r)] = bank
            for t in range(PACK):
                nodes = slice(t * P, (t + 1) * P)
                nc.tensor.matmul_mx(
                    out=bank[:, t, :],
                    lhsT=s_codes[:, nodes].bitcast(FP8X4),
                    lhsT_scale=s_scales[:, nodes],
                    rhs=x_codes[c][:, cols].bitcast(FP8X4),
                    rhs_scale=x_scales[c][:, cols],
                    start=True,
                    stop=True,
                )

        def shift(which, codes, scales, c, r):
            cols = slice(r * P, (r + 1) * P)
            bank = psum_o.tile([P, NODES], F32, name="zo%d_%d_%d" % (which, c, r), tag="zo")
            out_bank[(which, c, r)] = bank
            nc.tensor.matmul_mx(
                out=bank[:],
                lhsT=codes[c][:, cols].bitcast(FP8X4),
                lhsT_scale=scales[c][:, cols],
                rhs=s_codes[:].bitcast(FP8X4),
                rhs_scale=s_scales[:],
                start=True,
                stop=True,
            )

        def regroup_z(c, r):
            if r == 0:
                z_grp[c] = grp.tile([P, ROWS, P, PACK], BF16, name="z_grp%d" % c, tag="z_grp", align_bytes=64)
            nc.vector.tensor_copy(
                out=z_grp[c][:, r, :, :],
                in_=zt_bank[(c, r)][:].rearrange("p t g -> p g t"),
            )

        def quantise_z(c):
            z_codes[c] = keep.tile([P, CHUNK], U32, name="z_codes%d" % c, align_bytes=64)
            z_scales[c] = keep.tile([P, CHUNK], U8, name="z_scales%d" % c, align_bytes=64)
            nc.vector.quantize_mx(
                out=z_codes[c][:].bitcast(FP8X4),
                scales=z_scales[c][:],
                in_=z_grp[c][:].rearrange("p r m t -> p (r m t)"),
            )

        def empty(which, c, r, engine):
            if (which, c) not in out_stage:
                out_stage[(which, c)] = stage.tile([P, ROWS, NODES], F32, name="st%d_%d" % (which, c), tag="st")
            dst = out_stage[(which, c)][:, r, :]
            src = out_bank[(which, c, r)][:]
            if engine == "scalar":
                nc.scalar.copy(out=dst, in_=src)
            else:
                nc.vector.tensor_copy(out=dst, in_=src)

        def store(which, c, lo, hi):
            view = z1_view if which == 1 else z2_view
            nc.sync.dma_start(out=view[c][:, lo:hi, :], in_=out_stage[(which, c)][:, lo:hi, :])

        HALF = NODES // 2
        SPLIT = 80
        regroup_x(0, "vector", 0, P)
        nc.vector.tensor_copy(out=s_grp[:, :HALF, :], in_=s_raw[:, :, :HALF].rearrange("p t n -> p n t"))
        nc.scalar.copy(out=s_grp[:, HALF:, :], in_=s_raw[:, :, HALF:].rearrange("p t n -> p n t"))
        quantise_x(0)
        nc.vector.quantize_mx(
            out=s_codes[:].bitcast(FP8X4),
            scales=s_scales[:],
            in_=s_grp[:].rearrange("p n t -> p (n t)"),
        )
        regroup_x(1, "scalar", 0, 64)
        regroup_x(1, "vector", 64, P)
        for r in range(ROWS):
            shift_transposed(0, r)
            shift(1, x_codes, x_scales, 0, r)

        regroup_z(0, 0)
        quantise_x(1)
        regroup_x(2, "gpsimd", 0, 48)
        for r in range(ROWS):
            empty(1, 0, r, "scalar")
        store(1, 0, 0, ROWS)
        for r in range(ROWS):
            if r > 0:
                regroup_z(0, r)
            shift_transposed(1, r)
            shift(1, x_codes, x_scales, 1, r)
        for r in range(ROWS):
            empty(1, 1, r, "scalar")
        store(1, 1, 0, ROWS)
        quantise_z(0)
        regroup_x(2, "vector", 48, P)
        quantise_x(2)

        for c in range(1, NCHUNK):
            if c + 2 < NCHUNK:
                regroup_x(c + 2, "gpsimd", 0, (104 if c % 2 == 0 else SPLIT))
            for r in range(ROWS):
                shift(2, z_codes, z_scales, c - 1, r)
            for r in range(ROWS):
                empty(2, c - 1, r, "scalar")
            store(2, c - 1, 0, ROWS)
            for r in range(ROWS):
                regroup_z(c, r)
                if c + 1 < NCHUNK:
                    shift_transposed(c + 1, r)
                    shift(1, x_codes, x_scales, c + 1, r)
            if c + 1 < NCHUNK:
                helped = c % 2 == 0
                if helped:
                    empty(1, c + 1, 0, "vector")
                for r in range(ROWS):
                    if not (helped and r == 0):
                        empty(1, c + 1, r, "scalar")
                store(1, c + 1, 0, ROWS)
            if c + 2 < NCHUNK:
                regroup_x(c + 2, "vector", (104 if c % 2 == 0 else SPLIT), P)
            quantise_z(c)
            if c + 2 < NCHUNK:
                quantise_x(c + 2)

        last = NCHUNK - 1
        for r in range(ROWS):
            shift(2, z_codes, z_scales, last, r)
        empty(2, last, 0, "scalar")
        empty(2, last, 1, "vector")
        store(2, last, 0, 2)
        empty(2, last, 2, "scalar")
        empty(2, last, 3, "vector")
        store(2, last, 2, 4)
